import numpy as np
import ml_dtypes

BF16 = ml_dtypes.bfloat16


def bf(x):
    return np.asarray(x, np.float32).astype(BF16)


def f32(x):
    return np.asarray(x, np.float32)


def f64(x):
    return np.asarray(x).astype(np.float64)


def striped(idx):
    return np.tile(idx.reshape(-1, 16).T, (8, 1))


S, D, M, Q, B, K, N = 2048, 128, 512, 256, 128, 8, 1024


def setup_inputs():
    return {"table": bf(np.random.standard_normal((D, S))), "w_lab": bf(np.random.standard_normal((D, M)) / np.sqrt(D)), "embeds": bf(np.random.standard_normal((Q, N))), "w_emb": bf(np.random.standard_normal((Q, M)) / np.sqrt(Q)), "query": bf(np.random.standard_normal((Q, B))), "w_qry": bf(np.random.standard_normal((Q, M)) / np.sqrt(Q)), "b": f32(0.1 * np.random.standard_normal((M, 1))), "offs": striped(np.random.permutation(np.tile(np.arange(S), 2))[:N])}


def reference(table, w_lab, embeds, w_emb, query, w_qry, b, offs):
    idx = offs[:16].T.reshape(-1)
    lab = f64(w_lab).T @ f64(table)[:, idx]
    emb = f64(w_emb).T @ f64(embeds)
    qry = np.repeat(f64(w_qry).T @ f64(query), K, axis=1)
    return lab + emb + qry + f64(b)

@@ -1,0 +1,102 @@
+import concourse.mybir as mybir
+
+BF16, F32, U16 = mybir.dt.bfloat16, mybir.dt.float32, mybir.dt.uint16
+ADD = mybir.AluOpType.add
+
+P = 128
+LABELS = 2048
+FEATS = 512
+EMB = 256
+QUERIES = 128
+NEIGH = 8
+N = 1024
+PIECE = 512
+
+M_BLOCKS = FEATS // P
+K_BLOCKS = EMB // P
+Q_PIECE = PIECE // NEIGH
+
+FLOPS = 2 * FEATS * (N * (P + EMB) + QUERIES * EMB)
+
+
+def tile_rsaffdecoder_kernel(tc, table, w_lab, embeds, w_emb, query, w_qry, b, offs, out):
+    nc = tc.nc
+    with (
+        tc.tile_pool(name="held", bufs=1) as held,
+        tc.tile_pool(name="stage", bufs=4) as stage,
+        tc.psum_pool(name="psum", bufs=8) as psum,
+    ):
+        w_emb_sb = [held.tile([P, FEATS], BF16, name=f"w_emb_sb{k}") for k in range(K_BLOCKS)]
+        embeds_sb = [
+            [held.tile([P, PIECE], BF16, name=f"embeds_sb{piece}_{k}") for k in range(K_BLOCKS)] for piece in range(2)
+        ]
+        query_sb = held.tile([P, K_BLOCKS, QUERIES], BF16, name="query_sb")
+        w_qry_sb = held.tile([P, K_BLOCKS, FEATS], BF16, name="w_qry_sb")
+        offsets = held.tile([P, N // 16], U16, name="offsets")
+        w_lab_sb = held.tile([P, FEATS], BF16, name="w_lab_sb")
+        table_sb = held.tile([P, LABELS], BF16, name="table_sb")
+        bias = held.tile([P, M_BLOCKS], F32, name="bias")
+
+        for k in range(K_BLOCKS):
+            nc.sync.dma_start(w_emb_sb[k][:], w_emb[k * P : (k + 1) * P, :])
+            nc.sync.dma_start(embeds_sb[0][k][:], embeds[k * P : (k + 1) * P, 0:PIECE])
+        nc.sync.dma_start(query_sb[:], query.rearrange("(k p) q -> p k q", p=P))
+        nc.sync.dma_start(w_qry_sb[:], w_qry.rearrange("(k p) m -> p k m", p=P))
+        nc.sync.dma_start(offsets[:], offs)
+        nc.sync.dma_start(w_lab_sb[:], w_lab)
+        nc.sync.dma_start(table_sb[:], table)
+        for k in range(K_BLOCKS):
+            nc.sync.dma_start(embeds_sb[1][k][:], embeds[k * P : (k + 1) * P, PIECE:N])
+        with nc.allow_non_contiguous_dma(reason="bias: one float32 for each partition and block"):
+            nc.scalar.dma_start(bias[:], b.rearrange("(m p) o -> p (m o)", p=P))
+
+        qry_bias = held.tile([P, M_BLOCKS, QUERIES], F32, name="qry_bias")
+
+        def project_embeds(acc, piece, m, k, start, stop):
+            nc.tensor.matmul(acc[:], w_emb_sb[k][:, m * P : (m + 1) * P], embeds_sb[piece][k][:], start=start, stop=stop)
+
+        def project_labels(acc, piece, m, start, stop):
+            piece_offsets = offsets[:, piece * (PIECE // 16) : (piece + 1) * (PIECE // 16)]
+            nc.tensor.matmul(
+                acc[:], w_lab_sb[:, m * P : (m + 1) * P], table_sb[:].indirect(piece_offsets), start=start, stop=stop
+            )
+
+        def leave_psum(acc, piece, m):
+            staged = stage.tile([P, PIECE], F32, name="staged")
+            nc.vector.tensor_tensor(
+                staged[:].rearrange("p (q n) -> p q n", n=NEIGH),
+                acc[:].rearrange("p (q n) -> p q n", n=NEIGH),
+                qry_bias[:, m, piece * Q_PIECE : (piece + 1) * Q_PIECE].unsqueeze(2).to_broadcast([P, Q_PIECE, NEIGH]),
+                ADD,
+            )
+            store = nc.sync if m % 2 == 0 else nc.scalar
+            store.dma_start(out[m * P : (m + 1) * P, piece * PIECE : (piece + 1) * PIECE], staged[:])
+
+        acc0 = [psum.tile([P, PIECE], F32, name=f"acc0_{m}", tag="bank") for m in range(M_BLOCKS)]
+        for k in range(K_BLOCKS):
+            for m in range(M_BLOCKS):
+                project_embeds(acc0[m], 0, m, k, start=(k == 0), stop=False)
+
+        for m in range(M_BLOCKS):
+            qry_ps = psum.tile([P, PIECE], F32, name="qry_ps", tag="bank")
+            for k in range(K_BLOCKS):
+                nc.tensor.matmul(
+                    qry_ps[:, 0:QUERIES],
+                    w_qry_sb[:, k, m * P : (m + 1) * P],
+                    query_sb[:, k, :],
+                    start=(k == 0),
+                    stop=(k == K_BLOCKS - 1),
+                )
+            nc.vector.tensor_scalar(qry_bias[:, m, :], qry_ps[:, 0:QUERIES], bias[:, m : m + 1], None, ADD)
+
+        for m in range(M_BLOCKS):
+            project_labels(acc0[m], 0, m, start=False, stop=True)
+            leave_psum(acc0[m], 0, m)
+        acc1 = [psum.tile([P, PIECE], F32, name=f"acc1_{m}", tag="bank") for m in range(M_BLOCKS)]
+        for m in range(M_BLOCKS):
+            project_labels(acc1[m], 1, m, start=True, stop=False)
+
+        for m in range(M_BLOCKS):
+            for k in range(K_BLOCKS):
+                project_embeds(acc1[m], 1, m, k, start=False, stop=(k == K_BLOCKS - 1))
+            leave_psum(acc1[m], 1, m)

@@ -15,6 +15,7 @@ PIECE = 512
 M_BLOCKS = FEATS // P
 K_BLOCKS = EMB // P
 Q_PIECE = PIECE // NEIGH
+WARM_UP = 6
 
 FLOPS = 2 * FEATS * (N * (P + EMB) + QUERIES * EMB)
 
@@ -49,6 +50,12 @@ def tile_rsaffdecoder_kernel(tc, table, w_lab, embeds, w_emb, query, w_qry, b, o
             nc.sync.dma_start(embeds_sb[1][k][:], embeds[k * P : (k + 1) * P, PIECE:N])
         with nc.allow_non_contiguous_dma(reason="bias: one float32 for each partition and block"):
             nc.scalar.dma_start(bias[:], b.rearrange("(m p) o -> p (m o)", p=P))
+
+        zeros = held.tile([P, PIECE], BF16, name="zeros")
+        nc.vector.memset(zeros[:], 0.0)
+        warm_ps = psum.tile([P, PIECE], F32, name="warm_ps", tag="bank")
+        for i in range(WARM_UP):
+            nc.tensor.matmul(warm_ps[:], zeros[:, 0:P], zeros[:], start=True, stop=True)
 
         qry_bias = held.tile([P, M_BLOCKS, QUERIES], F32, name="qry_bias")
 

@@ -15,7 +15,7 @@ PIECE = 512
 M_BLOCKS = FEATS // P
 K_BLOCKS = EMB // P
 Q_PIECE = PIECE // NEIGH
-WARM_UP = 6
+WARM_UP = 16
 
 FLOPS = 2 * FEATS * (N * (P + EMB) + QUERIES * EMB)
 
@@ -51,11 +51,11 @@ def tile_rsaffdecoder_kernel(tc, table, w_lab, embeds, w_emb, query, w_qry, b, o
         with nc.allow_non_contiguous_dma(reason="bias: one float32 for each partition and block"):
             nc.scalar.dma_start(bias[:], b.rearrange("(m p) o -> p (m o)", p=P))
 
-        zeros = held.tile([P, PIECE], BF16, name="zeros")
+        zeros = held.tile([P, P], BF16, name="zeros")
         nc.vector.memset(zeros[:], 0.0)
         warm_ps = psum.tile([P, PIECE], F32, name="warm_ps", tag="bank")
         for i in range(WARM_UP):
-            nc.tensor.matmul(warm_ps[:], zeros[:, 0:P], zeros[:], start=True, stop=True)
+            nc.tensor.matmul(warm_ps[:, 0:P], zeros[:], zeros[:], start=True, stop=True)
 
         qry_bias = held.tile([P, M_BLOCKS, QUERIES], F32, name="qry_bias")
 

@@ -14,8 +14,10 @@ PIECE = 512
 
 M_BLOCKS = FEATS // P
 K_BLOCKS = EMB // P
+PIECES = N // PIECE
 Q_PIECE = PIECE // NEIGH
 WARM_UP = 16
+EARLY = 7
 
 FLOPS = 2 * FEATS * (N * (P + EMB) + QUERIES * EMB)
 
@@ -24,12 +26,12 @@ def tile_rsaffdecoder_kernel(tc, table, w_lab, embeds, w_emb, query, w_qry, b, o
     nc = tc.nc
     with (
         tc.tile_pool(name="held", bufs=1) as held,
-        tc.tile_pool(name="stage", bufs=4) as stage,
+        tc.tile_pool(name="stage", bufs=8) as stage,
         tc.psum_pool(name="psum", bufs=8) as psum,
     ):
         w_emb_sb = [held.tile([P, FEATS], BF16, name=f"w_emb_sb{k}") for k in range(K_BLOCKS)]
         embeds_sb = [
-            [held.tile([P, PIECE], BF16, name=f"embeds_sb{piece}_{k}") for k in range(K_BLOCKS)] for piece in range(2)
+            [held.tile([P, PIECE], BF16, name=f"embeds_sb{piece}_{k}") for k in range(K_BLOCKS)] for piece in range(PIECES)
         ]
         query_sb = held.tile([P, K_BLOCKS, QUERIES], BF16, name="query_sb")
         w_qry_sb = held.tile([P, K_BLOCKS, FEATS], BF16, name="w_qry_sb")
@@ -43,11 +45,11 @@ def tile_rsaffdecoder_kernel(tc, table, w_lab, embeds, w_emb, query, w_qry, b, o
             nc.sync.dma_start(embeds_sb[0][k][:], embeds[k * P : (k + 1) * P, 0:PIECE])
         nc.sync.dma_start(query_sb[:], query.rearrange("(k p) q -> p k q", p=P))
         nc.sync.dma_start(w_qry_sb[:], w_qry.rearrange("(k p) m -> p k m", p=P))
+        for k in range(K_BLOCKS):
+            nc.sync.dma_start(embeds_sb[1][k][:], embeds[k * P : (k + 1) * P, PIECE:N])
         nc.sync.dma_start(offsets[:], offs)
         nc.sync.dma_start(w_lab_sb[:], w_lab)
         nc.sync.dma_start(table_sb[:], table)
-        for k in range(K_BLOCKS):
-            nc.sync.dma_start(embeds_sb[1][k][:], embeds[k * P : (k + 1) * P, PIECE:N])
         with nc.allow_non_contiguous_dma(reason="bias: one float32 for each partition and block"):
             nc.scalar.dma_start(bias[:], b.rearrange("(m p) o -> p (m o)", p=P))
 
@@ -79,31 +81,42 @@ def tile_rsaffdecoder_kernel(tc, table, w_lab, embeds, w_emb, query, w_qry, b, o
             store = nc.sync if m % 2 == 0 else nc.scalar
             store.dma_start(out[m * P : (m + 1) * P, piece * PIECE : (piece + 1) * PIECE], staged[:])
 
-        acc0 = [psum.tile([P, PIECE], F32, name=f"acc0_{m}", tag="bank") for m in range(M_BLOCKS)]
-        for k in range(K_BLOCKS):
-            for m in range(M_BLOCKS):
-                project_embeds(acc0[m], 0, m, k, start=(k == 0), stop=False)
+        banks = [(piece, m) for piece in range(PIECES) for m in range(M_BLOCKS)]
+        acc = {}
 
+        for piece, m in banks[:M_BLOCKS]:
+            acc[piece, m] = psum.tile([P, PIECE], F32, name=f"acc{piece}_{m}", tag="bank")
+        for k in range(K_BLOCKS):
+            for piece, m in banks[:M_BLOCKS]:
+                project_embeds(acc[piece, m], piece, m, k, start=(k == 0), stop=False)
+
+        qry_ps = psum.tile([P, M_BLOCKS, QUERIES], F32, name="qry_ps", tag="bank")
         for m in range(M_BLOCKS):
-            qry_ps = psum.tile([P, PIECE], F32, name="qry_ps", tag="bank")
             for k in range(K_BLOCKS):
                 nc.tensor.matmul(
-                    qry_ps[:, 0:QUERIES],
+                    qry_ps[:, m, :],
                     w_qry_sb[:, k, m * P : (m + 1) * P],
                     query_sb[:, k, :],
                     start=(k == 0),
                     stop=(k == K_BLOCKS - 1),
                 )
-            nc.vector.tensor_scalar(qry_bias[:, m, :], qry_ps[:, 0:QUERIES], bias[:, m : m + 1], None, ADD)
+        nc.vector.tensor_tensor(
+            qry_bias[:], qry_ps[:], bias[:].unsqueeze(2).to_broadcast([P, M_BLOCKS, QUERIES]), ADD
+        )
 
-        for m in range(M_BLOCKS):
-            project_labels(acc0[m], 0, m, start=False, stop=True)
-            leave_psum(acc0[m], 0, m)
-        acc1 = [psum.tile([P, PIECE], F32, name=f"acc1_{m}", tag="bank") for m in range(M_BLOCKS)]
-        for m in range(M_BLOCKS):
-            project_labels(acc1[m], 1, m, start=True, stop=False)
-
-        for m in range(M_BLOCKS):
+        for piece, m in banks[M_BLOCKS:EARLY]:
+            acc[piece, m] = psum.tile([P, PIECE], F32, name=f"acc{piece}_{m}", tag="bank")
             for k in range(K_BLOCKS):
-                project_embeds(acc1[m], 1, m, k, start=False, stop=(k == K_BLOCKS - 1))
-            leave_psum(acc1[m], 1, m)
+                project_embeds(acc[piece, m], piece, m, k, start=(k == 0), stop=False)
+
+        for piece, m in banks[:EARLY]:
+            project_labels(acc[piece, m], piece, m, start=False, stop=True)
+            leave_psum(acc[piece, m], piece, m)
+        for piece, m in banks[EARLY:]:
+            acc[piece, m] = psum.tile([P, PIECE], F32, name=f"acc{piece}_{m}", tag="bank")
+            project_labels(acc[piece, m], piece, m, start=True, stop=False)
+
+        for piece, m in banks[EARLY:]:
+            for k in range(K_BLOCKS):
+                project_embeds(acc[piece, m], piece, m, k, start=False, stop=(k == K_BLOCKS - 1))
+            leave_psum(acc[piece, m], piece, m)

@@ -16,6 +16,7 @@ M_BLOCKS = FEATS // P
 K_BLOCKS = EMB // P
 PIECES = N // PIECE
 Q_PIECE = PIECE // NEIGH
+SQUARE = 32
 WARM_UP = 16
 EARLY = 7
 
@@ -38,7 +39,6 @@ def tile_rsaffdecoder_kernel(tc, table, w_lab, embeds, w_emb, query, w_qry, b, o
         offsets = held.tile([P, N // 16], U16, name="offsets")
         w_lab_sb = held.tile([P, FEATS], BF16, name="w_lab_sb")
         table_sb = held.tile([P, LABELS], BF16, name="table_sb")
-        bias = held.tile([P, M_BLOCKS], F32, name="bias")
 
         for k in range(K_BLOCKS):
             nc.sync.dma_start(w_emb_sb[k][:], w_emb[k * P : (k + 1) * P, :])
@@ -50,8 +50,14 @@ def tile_rsaffdecoder_kernel(tc, table, w_lab, embeds, w_emb, query, w_qry, b, o
         nc.sync.dma_start(offsets[:], offs)
         nc.sync.dma_start(w_lab_sb[:], w_lab)
         nc.sync.dma_start(table_sb[:], table)
-        with nc.allow_non_contiguous_dma(reason="bias: one float32 for each partition and block"):
-            nc.scalar.dma_start(bias[:], b.rearrange("(m p) o -> p (m o)", p=P))
+
+        b_runs = held.tile([P, SQUARE], F32, name="b_runs", align_bytes=64)
+        bias = held.tile([P, SQUARE], F32, name="bias", align_bytes=64)
+        nc.vector.memset(b_runs[:], 0.0)
+        b_by_square = b.rearrange("(m s i) o -> s m (i o)", s=P // SQUARE, i=SQUARE)
+        for s in range(P // SQUARE):
+            nc.scalar.dma_start(b_runs[s * SQUARE : s * SQUARE + M_BLOCKS, :], b_by_square[s])
+        nc.vector.transpose(bias[:], b_runs[:])
 
         zeros = held.tile([P, P], BF16, name="zeros")
         nc.vector.memset(zeros[:], 0.0)
@@ -101,7 +107,7 @@ def tile_rsaffdecoder_kernel(tc, table, w_lab, embeds, w_emb, query, w_qry, b, o
                     stop=(k == K_BLOCKS - 1),
                 )
         nc.vector.tensor_tensor(
-            qry_bias[:], qry_ps[:], bias[:].unsqueeze(2).to_broadcast([P, M_BLOCKS, QUERIES]), ADD
+            qry_bias[:], qry_ps[:], bias[:, 0:M_BLOCKS].unsqueeze(2).to_broadcast([P, M_BLOCKS, QUERIES]), ADD
         )
 
         for piece, m in banks[M_BLOCKS:EARLY]:

@@ -18,7 +18,7 @@ PIECES = N // PIECE
 Q_PIECE = PIECE // NEIGH
 SQUARE = 32
 WARM_UP = 16
-EARLY = 7
+EARLY = 6
 
 FLOPS = 2 * FEATS * (N * (P + EMB) + QUERIES * EMB)
 

@@ -11,14 +11,17 @@ QUERIES = 128
 NEIGH = 8
 N = 1024
 PIECE = 512
+SQUARE = 32
 
 M_BLOCKS = FEATS // P
 K_BLOCKS = EMB // P
 PIECES = N // PIECE
-Q_PIECE = PIECE // NEIGH
-SQUARE = 32
+PSUM_BANKS = 8
+
+N_BANKS = PIECES * M_BLOCKS
+EARLY = N_BANKS - 1
+LATE_PARTS = 2
 WARM_UP = 16
-EARLY = 6
 
 FLOPS = 2 * FEATS * (N * (P + EMB) + QUERIES * EMB)
 
@@ -27,12 +30,13 @@ def tile_rsaffdecoder_kernel(tc, table, w_lab, embeds, w_emb, query, w_qry, b, o
     nc = tc.nc
     with (
         tc.tile_pool(name="held", bufs=1) as held,
-        tc.tile_pool(name="stage", bufs=8) as stage,
-        tc.psum_pool(name="psum", bufs=8) as psum,
+        tc.tile_pool(name="stage", bufs=EARLY + (N_BANKS - EARLY) * LATE_PARTS) as stage,
+        tc.psum_pool(name="psum", bufs=PSUM_BANKS) as psum,
     ):
         w_emb_sb = [held.tile([P, FEATS], BF16, name=f"w_emb_sb{k}") for k in range(K_BLOCKS)]
         embeds_sb = [
-            [held.tile([P, PIECE], BF16, name=f"embeds_sb{piece}_{k}") for k in range(K_BLOCKS)] for piece in range(PIECES)
+            [held.tile([P, PIECE], BF16, name=f"embeds_sb{piece}_{k}") for k in range(K_BLOCKS)]
+            for piece in range(PIECES)
         ]
         query_sb = held.tile([P, K_BLOCKS, QUERIES], BF16, name="query_sb")
         w_qry_sb = held.tile([P, K_BLOCKS, FEATS], BF16, name="w_qry_sb")
@@ -51,6 +55,12 @@ def tile_rsaffdecoder_kernel(tc, table, w_lab, embeds, w_emb, query, w_qry, b, o
         nc.sync.dma_start(w_lab_sb[:], w_lab)
         nc.sync.dma_start(table_sb[:], table)
 
+        zeros = held.tile([P, P], BF16, name="zeros")
+        nc.vector.memset(zeros[:], 0.0)
+        warm_ps = psum.tile([P, PIECE], F32, name="warm_ps", tag="bank")
+        for i in range(WARM_UP):
+            nc.tensor.matmul(warm_ps[:, 0:P], zeros[:], zeros[:], start=True, stop=True)
+
         b_runs = held.tile([P, SQUARE], F32, name="b_runs", align_bytes=64)
         bias = held.tile([P, SQUARE], F32, name="bias", align_bytes=64)
         nc.vector.memset(b_runs[:], 0.0)
@@ -59,42 +69,49 @@ def tile_rsaffdecoder_kernel(tc, table, w_lab, embeds, w_emb, query, w_qry, b, o
             nc.scalar.dma_start(b_runs[s * SQUARE : s * SQUARE + M_BLOCKS, :], b_by_square[s])
         nc.vector.transpose(bias[:], b_runs[:])
 
-        zeros = held.tile([P, P], BF16, name="zeros")
-        nc.vector.memset(zeros[:], 0.0)
-        warm_ps = psum.tile([P, PIECE], F32, name="warm_ps", tag="bank")
-        for i in range(WARM_UP):
-            nc.tensor.matmul(warm_ps[:, 0:P], zeros[:], zeros[:], start=True, stop=True)
-
-        qry_bias = held.tile([P, M_BLOCKS, QUERIES], F32, name="qry_bias")
-
-        def project_embeds(acc, piece, m, k, start, stop):
-            nc.tensor.matmul(acc[:], w_emb_sb[k][:, m * P : (m + 1) * P], embeds_sb[piece][k][:], start=start, stop=stop)
-
-        def project_labels(acc, piece, m, start, stop):
-            piece_offsets = offsets[:, piece * (PIECE // 16) : (piece + 1) * (PIECE // 16)]
-            nc.tensor.matmul(
-                acc[:], w_lab_sb[:, m * P : (m + 1) * P], table_sb[:].indirect(piece_offsets), start=start, stop=stop
-            )
-
-        def leave_psum(acc, piece, m):
-            staged = stage.tile([P, PIECE], F32, name="staged")
-            nc.vector.tensor_tensor(
-                staged[:].rearrange("p (q n) -> p q n", n=NEIGH),
-                acc[:].rearrange("p (q n) -> p q n", n=NEIGH),
-                qry_bias[:, m, piece * Q_PIECE : (piece + 1) * Q_PIECE].unsqueeze(2).to_broadcast([P, Q_PIECE, NEIGH]),
-                ADD,
-            )
-            store = nc.sync if m % 2 == 0 else nc.scalar
-            store.dma_start(out[m * P : (m + 1) * P, piece * PIECE : (piece + 1) * PIECE], staged[:])
-
         banks = [(piece, m) for piece in range(PIECES) for m in range(M_BLOCKS)]
         acc = {}
+        qry_bias = held.tile([P, M_BLOCKS, QUERIES], F32, name="qry_bias")
+
+        def open_bank(piece, m):
+            acc[piece, m] = psum.tile([P, PIECE], F32, name=f"acc{piece}_{m}", tag="bank")
+
+        def project_embeds(piece, m, k, start, stop):
+            nc.tensor.matmul(
+                acc[piece, m][:], w_emb_sb[k][:, m * P : (m + 1) * P], embeds_sb[piece][k][:], start=start, stop=stop
+            )
+
+        def project_labels(piece, m, start, stop):
+            piece_offsets = offsets[:, piece * (PIECE // 16) : (piece + 1) * (PIECE // 16)]
+            nc.tensor.matmul(
+                acc[piece, m][:],
+                w_lab_sb[:, m * P : (m + 1) * P],
+                table_sb[:].indirect(piece_offsets),
+                start=start,
+                stop=stop,
+            )
+
+        def leave_psum(piece, m, parts):
+            width = PIECE // parts
+            for part in range(parts):
+                first = piece * PIECE + part * width
+                staged = stage.tile([P, width], F32, name="staged")
+                nc.vector.tensor_tensor(
+                    staged[:].rearrange("p (q n) -> p q n", n=NEIGH),
+                    acc[piece, m][:, part * width : (part + 1) * width].rearrange("p (q n) -> p q n", n=NEIGH),
+                    qry_bias[:, m, first // NEIGH : (first + width) // NEIGH]
+                    .unsqueeze(2)
+                    .to_broadcast([P, width // NEIGH, NEIGH]),
+                    ADD,
+                )
+                store = nc.sync if (m + part) % 2 == 0 else nc.scalar
+                store.dma_start(out[m * P : (m + 1) * P, first : first + width], staged[:])
 
         for piece, m in banks[:M_BLOCKS]:
-            acc[piece, m] = psum.tile([P, PIECE], F32, name=f"acc{piece}_{m}", tag="bank")
+            open_bank(piece, m)
         for k in range(K_BLOCKS):
             for piece, m in banks[:M_BLOCKS]:
-                project_embeds(acc[piece, m], piece, m, k, start=(k == 0), stop=False)
+                project_embeds(piece, m, k, start=(k == 0), stop=False)
 
         qry_ps = psum.tile([P, M_BLOCKS, QUERIES], F32, name="qry_ps", tag="bank")
         for m in range(M_BLOCKS):
@@ -111,18 +128,18 @@ def tile_rsaffdecoder_kernel(tc, table, w_lab, embeds, w_emb, query, w_qry, b, o
         )
 
         for piece, m in banks[M_BLOCKS:EARLY]:
-            acc[piece, m] = psum.tile([P, PIECE], F32, name=f"acc{piece}_{m}", tag="bank")
+            open_bank(piece, m)
             for k in range(K_BLOCKS):
-                project_embeds(acc[piece, m], piece, m, k, start=(k == 0), stop=False)
+                project_embeds(piece, m, k, start=(k == 0), stop=False)
 
         for piece, m in banks[:EARLY]:
-            project_labels(acc[piece, m], piece, m, start=False, stop=True)
-            leave_psum(acc[piece, m], piece, m)
+            project_labels(piece, m, start=False, stop=True)
+            leave_psum(piece, m, parts=1)
         for piece, m in banks[EARLY:]:
-            acc[piece, m] = psum.tile([P, PIECE], F32, name=f"acc{piece}_{m}", tag="bank")
-            project_labels(acc[piece, m], piece, m, start=True, stop=False)
+            open_bank(piece, m)
+            project_labels(piece, m, start=True, stop=False)
 
         for piece, m in banks[EARLY:]:
             for k in range(K_BLOCKS):
-                project_embeds(acc[piece, m], piece, m, k, start=False, stop=(k == K_BLOCKS - 1))
-            leave_psum(acc[piece, m], piece, m)
+                project_embeds(piece, m, k, start=False, stop=(k == K_BLOCKS - 1))
+            leave_psum(piece, m, parts=LATE_PARTS)

@@ -104,8 +104,7 @@ def tile_rsaffdecoder_kernel(tc, table, w_lab, embeds, w_emb, query, w_qry, b, o
                     .to_broadcast([P, width // NEIGH, NEIGH]),
                     ADD,
                 )
-                store = nc.sync if (m + part) % 2 == 0 else nc.scalar
-                store.dma_start(out[m * P : (m + 1) * P, first : first + width], staged[:])
+                nc.sync.dma_start(out[m * P : (m + 1) * P, first : first + width], staged[:])
 
         for piece, m in banks[:M_BLOCKS]:
             open_bank(piece, m)

@@ -11,7 +11,6 @@ QUERIES = 128
 NEIGH = 8
 N = 1024
 PIECE = 512
-SQUARE = 32
 
 M_BLOCKS = FEATS // P
 K_BLOCKS = EMB // P
@@ -34,23 +33,22 @@ def tile_rsaffdecoder_kernel(tc, table, w_lab, embeds, w_emb, query, w_qry, b, o
         tc.psum_pool(name="psum", bufs=PSUM_BANKS) as psum,
     ):
         w_emb_sb = [held.tile([P, FEATS], BF16, name=f"w_emb_sb{k}") for k in range(K_BLOCKS)]
-        embeds_sb = [
-            [held.tile([P, PIECE], BF16, name=f"embeds_sb{piece}_{k}") for k in range(K_BLOCKS)]
-            for piece in range(PIECES)
-        ]
+        embeds0_sb = [held.tile([P, PIECE], BF16, name=f"embeds0_sb{k}") for k in range(K_BLOCKS)]
+        embeds1_sb = held.tile([P, K_BLOCKS, PIECE], BF16, name="embeds1_sb")
         query_sb = held.tile([P, K_BLOCKS, QUERIES], BF16, name="query_sb")
         w_qry_sb = held.tile([P, K_BLOCKS, FEATS], BF16, name="w_qry_sb")
+        bias = held.tile([P, M_BLOCKS], F32, name="bias")
         offsets = held.tile([P, N // 16], U16, name="offsets")
         w_lab_sb = held.tile([P, FEATS], BF16, name="w_lab_sb")
         table_sb = held.tile([P, LABELS], BF16, name="table_sb")
 
         for k in range(K_BLOCKS):
             nc.sync.dma_start(w_emb_sb[k][:], w_emb[k * P : (k + 1) * P, :])
-            nc.sync.dma_start(embeds_sb[0][k][:], embeds[k * P : (k + 1) * P, 0:PIECE])
+            nc.sync.dma_start(embeds0_sb[k][:], embeds[k * P : (k + 1) * P, 0:PIECE])
         nc.sync.dma_start(query_sb[:], query.rearrange("(k p) q -> p k q", p=P))
         nc.sync.dma_start(w_qry_sb[:], w_qry.rearrange("(k p) m -> p k m", p=P))
-        for k in range(K_BLOCKS):
-            nc.sync.dma_start(embeds_sb[1][k][:], embeds[k * P : (k + 1) * P, PIECE:N])
+        nc.sync.dma_start(embeds1_sb[:], embeds[:, PIECE:N].rearrange("(k p) j -> p k j", p=P))
+        nc.sync.dma_start(bias[:], b.rearrange("(p m) o -> p (m o)", m=M_BLOCKS))
         nc.sync.dma_start(offsets[:], offs)
         nc.sync.dma_start(w_lab_sb[:], w_lab)
         nc.sync.dma_start(table_sb[:], table)
@@ -61,31 +59,27 @@ def tile_rsaffdecoder_kernel(tc, table, w_lab, embeds, w_emb, query, w_qry, b, o
         for i in range(WARM_UP):
             nc.tensor.matmul(warm_ps[:, 0:P], zeros[:], zeros[:], start=True, stop=True)
 
-        b_runs = held.tile([P, SQUARE], F32, name="b_runs", align_bytes=64)
-        bias = held.tile([P, SQUARE], F32, name="bias", align_bytes=64)
-        nc.vector.memset(b_runs[:], 0.0)
-        b_by_square = b.rearrange("(m s i) o -> s m (i o)", s=P // SQUARE, i=SQUARE)
-        for s in range(P // SQUARE):
-            nc.scalar.dma_start(b_runs[s * SQUARE : s * SQUARE + M_BLOCKS, :], b_by_square[s])
-        nc.vector.transpose(bias[:], b_runs[:])
-
         banks = [(piece, m) for piece in range(PIECES) for m in range(M_BLOCKS)]
         acc = {}
         qry_bias = held.tile([P, M_BLOCKS, QUERIES], F32, name="qry_bias")
+
+        def block(m):
+            return slice(m, FEATS, M_BLOCKS)
+
+        out_blocks = out.rearrange("(p m) j -> m p j", m=M_BLOCKS)
 
         def open_bank(piece, m):
             acc[piece, m] = psum.tile([P, PIECE], F32, name=f"acc{piece}_{m}", tag="bank")
 
         def project_embeds(piece, m, k, start, stop):
-            nc.tensor.matmul(
-                acc[piece, m][:], w_emb_sb[k][:, m * P : (m + 1) * P], embeds_sb[piece][k][:], start=start, stop=stop
-            )
+            moving = embeds0_sb[k][:] if piece == 0 else embeds1_sb[:, k, :]
+            nc.tensor.matmul(acc[piece, m][:], w_emb_sb[k][:, block(m)], moving, start=start, stop=stop)
 
         def project_labels(piece, m, start, stop):
             piece_offsets = offsets[:, piece * (PIECE // 16) : (piece + 1) * (PIECE // 16)]
             nc.tensor.matmul(
                 acc[piece, m][:],
-                w_lab_sb[:, m * P : (m + 1) * P],
+                w_lab_sb[:, block(m)],
                 table_sb[:].indirect(piece_offsets),
                 start=start,
                 stop=stop,
@@ -104,7 +98,7 @@ def tile_rsaffdecoder_kernel(tc, table, w_lab, embeds, w_emb, query, w_qry, b, o
                     .to_broadcast([P, width // NEIGH, NEIGH]),
                     ADD,
                 )
-                nc.sync.dma_start(out[m * P : (m + 1) * P, first : first + width], staged[:])
+                nc.sync.dma_start(out_blocks[m][:, first : first + width], staged[:])
 
         for piece, m in banks[:M_BLOCKS]:
             open_bank(piece, m)
@@ -117,13 +111,13 @@ def tile_rsaffdecoder_kernel(tc, table, w_lab, embeds, w_emb, query, w_qry, b, o
             for k in range(K_BLOCKS):
                 nc.tensor.matmul(
                     qry_ps[:, m, :],
-                    w_qry_sb[:, k, m * P : (m + 1) * P],
+                    w_qry_sb[:, k, block(m)],
                     query_sb[:, k, :],
                     start=(k == 0),
                     stop=(k == K_BLOCKS - 1),
                 )
         nc.vector.tensor_tensor(
-            qry_bias[:], qry_ps[:], bias[:, 0:M_BLOCKS].unsqueeze(2).to_broadcast([P, M_BLOCKS, QUERIES]), ADD
+            qry_bias[:], qry_ps[:], bias[:].unsqueeze(2).to_broadcast([P, M_BLOCKS, QUERIES]), ADD
         )
 
         for piece, m in banks[M_BLOCKS:EARLY]:

@@ -13,6 +13,9 @@ N = 1024
 PIECE = 512
 
 M_BLOCKS = FEATS // P
+HALVES = 2
+HALF = FEATS // HALVES
+STEP = M_BLOCKS // HALVES
 K_BLOCKS = EMB // P
 PIECES = N // PIECE
 PSUM_BANKS = 8
@@ -33,22 +36,32 @@ def tile_rsaffdecoder_kernel(tc, table, w_lab, embeds, w_emb, query, w_qry, b, o
         tc.psum_pool(name="psum", bufs=PSUM_BANKS) as psum,
     ):
         w_emb_sb = [held.tile([P, FEATS], BF16, name=f"w_emb_sb{k}") for k in range(K_BLOCKS)]
-        embeds0_sb = [held.tile([P, PIECE], BF16, name=f"embeds0_sb{k}") for k in range(K_BLOCKS)]
-        embeds1_sb = held.tile([P, K_BLOCKS, PIECE], BF16, name="embeds1_sb")
-        query_sb = held.tile([P, K_BLOCKS, QUERIES], BF16, name="query_sb")
-        w_qry_sb = held.tile([P, K_BLOCKS, FEATS], BF16, name="w_qry_sb")
-        bias = held.tile([P, M_BLOCKS], F32, name="bias")
+        embeds_sb = [
+            [held.tile([P, PIECE], BF16, name=f"embeds_sb{piece}_{k}") for k in range(K_BLOCKS)]
+            for piece in range(PIECES)
+        ]
+        query_sb = [held.tile([P, QUERIES], BF16, name=f"query_sb{k}") for k in range(K_BLOCKS)]
+        w_qry_sb = [held.tile([P, FEATS], BF16, name=f"w_qry_sb{k}") for k in range(K_BLOCKS)]
+        bias = held.tile([P, HALVES, STEP], F32, name="bias")
         offsets = held.tile([P, N // 16], U16, name="offsets")
         w_lab_sb = held.tile([P, FEATS], BF16, name="w_lab_sb")
         table_sb = held.tile([P, LABELS], BF16, name="table_sb")
 
+        def load_rows(tile, array, k, columns):
+            nc.sync.dma_start(tile[:], array[k * P : (k + 1) * P, columns])
+
+        load_rows(embeds_sb[0][0], embeds, 0, slice(0, PIECE))
+        for h in range(HALVES):
+            half = slice(h * HALF, (h + 1) * HALF)
+            nc.sync.dma_start(w_emb_sb[0][:, half], w_emb[0:P, half])
+        load_rows(embeds_sb[0][1], embeds, 1, slice(0, PIECE))
+        load_rows(w_emb_sb[1], w_emb, 1, slice(0, FEATS))
         for k in range(K_BLOCKS):
-            nc.sync.dma_start(w_emb_sb[k][:], w_emb[k * P : (k + 1) * P, :])
-            nc.sync.dma_start(embeds0_sb[k][:], embeds[k * P : (k + 1) * P, 0:PIECE])
-        nc.sync.dma_start(query_sb[:], query.rearrange("(k p) q -> p k q", p=P))
-        nc.sync.dma_start(w_qry_sb[:], w_qry.rearrange("(k p) m -> p k m", p=P))
-        nc.sync.dma_start(embeds1_sb[:], embeds[:, PIECE:N].rearrange("(k p) j -> p k j", p=P))
-        nc.sync.dma_start(bias[:], b.rearrange("(p m) o -> p (m o)", m=M_BLOCKS))
+            load_rows(query_sb[k], query, k, slice(0, QUERIES))
+            load_rows(w_qry_sb[k], w_qry, k, slice(0, FEATS))
+        for k in range(K_BLOCKS):
+            load_rows(embeds_sb[1][k], embeds, k, slice(PIECE, N))
+        nc.sync.dma_start(bias[:], b.rearrange("(h p s) o -> p h (s o)", h=HALVES, s=STEP))
         nc.sync.dma_start(offsets[:], offs)
         nc.sync.dma_start(w_lab_sb[:], w_lab)
         nc.sync.dma_start(table_sb[:], table)
@@ -64,16 +77,18 @@ def tile_rsaffdecoder_kernel(tc, table, w_lab, embeds, w_emb, query, w_qry, b, o
         qry_bias = held.tile([P, M_BLOCKS, QUERIES], F32, name="qry_bias")
 
         def block(m):
-            return slice(m, FEATS, M_BLOCKS)
+            first = (m // STEP) * HALF + m % STEP
+            return slice(first, (m // STEP + 1) * HALF, STEP)
 
-        out_blocks = out.rearrange("(p m) j -> m p j", m=M_BLOCKS)
+        out_blocks = out.rearrange("(h p s) j -> h s p j", h=HALVES, s=STEP)
 
         def open_bank(piece, m):
             acc[piece, m] = psum.tile([P, PIECE], F32, name=f"acc{piece}_{m}", tag="bank")
 
         def project_embeds(piece, m, k, start, stop):
-            moving = embeds0_sb[k][:] if piece == 0 else embeds1_sb[:, k, :]
-            nc.tensor.matmul(acc[piece, m][:], w_emb_sb[k][:, block(m)], moving, start=start, stop=stop)
+            nc.tensor.matmul(
+                acc[piece, m][:], w_emb_sb[k][:, block(m)], embeds_sb[piece][k][:], start=start, stop=stop
+            )
 
         def project_labels(piece, m, start, stop):
             piece_offsets = offsets[:, piece * (PIECE // 16) : (piece + 1) * (PIECE // 16)]
@@ -98,7 +113,7 @@ def tile_rsaffdecoder_kernel(tc, table, w_lab, embeds, w_emb, query, w_qry, b, o
                     .to_broadcast([P, width // NEIGH, NEIGH]),
                     ADD,
                 )
-                nc.sync.dma_start(out_blocks[m][:, first : first + width], staged[:])
+                nc.sync.dma_start(out_blocks[m // STEP][m % STEP][:, first : first + width], staged[:])
 
         for piece, m in banks[:M_BLOCKS]:
             open_bank(piece, m)
@@ -111,13 +126,16 @@ def tile_rsaffdecoder_kernel(tc, table, w_lab, embeds, w_emb, query, w_qry, b, o
             for k in range(K_BLOCKS):
                 nc.tensor.matmul(
                     qry_ps[:, m, :],
-                    w_qry_sb[:, k, block(m)],
-                    query_sb[:, k, :],
+                    w_qry_sb[k][:, block(m)],
+                    query_sb[k][:],
                     start=(k == 0),
                     stop=(k == K_BLOCKS - 1),
                 )
         nc.vector.tensor_tensor(
-            qry_bias[:], qry_ps[:], bias[:].unsqueeze(2).to_broadcast([P, M_BLOCKS, QUERIES]), ADD
+            qry_bias[:],
+            qry_ps[:],
+            bias[:].rearrange("p h s -> p (h s)").unsqueeze(2).to_broadcast([P, M_BLOCKS, QUERIES]),
+            ADD,
         )
 
         for piece, m in banks[M_BLOCKS:EARLY]:

@@ -23,7 +23,7 @@ PSUM_BANKS = 8
 N_BANKS = PIECES * M_BLOCKS
 EARLY = N_BANKS - 1
 LATE_PARTS = 2
-WARM_UP = 16
+WARM_UP = 10
 
 FLOPS = 2 * FEATS * (N * (P + EMB) + QUERIES * EMB)
 

@@ -22,7 +22,7 @@ PSUM_BANKS = 8
 
 N_BANKS = PIECES * M_BLOCKS
 EARLY = N_BANKS - 1
-LATE_PARTS = 2
+END_PARTS = 2
 WARM_UP = 10
 
 FLOPS = 2 * FEATS * (N * (P + EMB) + QUERIES * EMB)
@@ -32,36 +32,31 @@ def tile_rsaffdecoder_kernel(tc, table, w_lab, embeds, w_emb, query, w_qry, b, o
     nc = tc.nc
     with (
         tc.tile_pool(name="held", bufs=1) as held,
-        tc.tile_pool(name="stage", bufs=EARLY + (N_BANKS - EARLY) * LATE_PARTS) as stage,
+        tc.tile_pool(name="stage", bufs=N_BANKS - 2 + 2 * END_PARTS) as stage,
         tc.psum_pool(name="psum", bufs=PSUM_BANKS) as psum,
     ):
         w_emb_sb = [held.tile([P, FEATS], BF16, name=f"w_emb_sb{k}") for k in range(K_BLOCKS)]
-        embeds_sb = [
-            [held.tile([P, PIECE], BF16, name=f"embeds_sb{piece}_{k}") for k in range(K_BLOCKS)]
-            for piece in range(PIECES)
-        ]
-        query_sb = [held.tile([P, QUERIES], BF16, name=f"query_sb{k}") for k in range(K_BLOCKS)]
-        w_qry_sb = [held.tile([P, FEATS], BF16, name=f"w_qry_sb{k}") for k in range(K_BLOCKS)]
-        bias = held.tile([P, HALVES, STEP], F32, name="bias")
+        embeds0_sb = [held.tile([P, PIECE], BF16, name=f"embeds0_sb{k}") for k in range(K_BLOCKS)]
+        embeds1_sb = held.tile([P, K_BLOCKS, PIECE], BF16, name="embeds1_sb")
+        query_sb = held.tile([P, K_BLOCKS, QUERIES], BF16, name="query_sb")
+        w_qry_sb = held.tile([P, K_BLOCKS, FEATS], BF16, name="w_qry_sb")
+        bias = [held.tile([P, STEP], F32, name=f"bias{h}") for h in range(HALVES)]
         offsets = held.tile([P, N // 16], U16, name="offsets")
         w_lab_sb = held.tile([P, FEATS], BF16, name="w_lab_sb")
         table_sb = held.tile([P, LABELS], BF16, name="table_sb")
 
-        def load_rows(tile, array, k, columns):
-            nc.sync.dma_start(tile[:], array[k * P : (k + 1) * P, columns])
-
-        load_rows(embeds_sb[0][0], embeds, 0, slice(0, PIECE))
+        nc.sync.dma_start(embeds0_sb[0][:], embeds[0:P, 0:PIECE])
         for h in range(HALVES):
             half = slice(h * HALF, (h + 1) * HALF)
             nc.sync.dma_start(w_emb_sb[0][:, half], w_emb[0:P, half])
-        load_rows(embeds_sb[0][1], embeds, 1, slice(0, PIECE))
-        load_rows(w_emb_sb[1], w_emb, 1, slice(0, FEATS))
+        nc.sync.dma_start(embeds0_sb[1][:], embeds[P:EMB, 0:PIECE])
+        nc.sync.dma_start(w_emb_sb[1][:], w_emb[P:EMB, :])
+        nc.sync.dma_start(query_sb[:], query.rearrange("(p k) q -> p k q", k=K_BLOCKS))
+        nc.sync.dma_start(w_qry_sb[:], w_qry.rearrange("(p k) f -> p k f", k=K_BLOCKS))
         for k in range(K_BLOCKS):
-            load_rows(query_sb[k], query, k, slice(0, QUERIES))
-            load_rows(w_qry_sb[k], w_qry, k, slice(0, FEATS))
-        for k in range(K_BLOCKS):
-            load_rows(embeds_sb[1][k], embeds, k, slice(PIECE, N))
-        nc.sync.dma_start(bias[:], b.rearrange("(h p s) o -> p h (s o)", h=HALVES, s=STEP))
+            nc.sync.dma_start(embeds1_sb[:, k, :], embeds[k * P : (k + 1) * P, PIECE:N])
+        for h in range(HALVES):
+            nc.sync.dma_start(bias[h][:], b[h * HALF : (h + 1) * HALF, :].rearrange("(p s) o -> p (s o)", s=STEP))
         nc.sync.dma_start(offsets[:], offs)
         nc.sync.dma_start(w_lab_sb[:], w_lab)
         nc.sync.dma_start(table_sb[:], table)
@@ -86,9 +81,8 @@ def tile_rsaffdecoder_kernel(tc, table, w_lab, embeds, w_emb, query, w_qry, b, o
             acc[piece, m] = psum.tile([P, PIECE], F32, name=f"acc{piece}_{m}", tag="bank")
 
         def project_embeds(piece, m, k, start, stop):
-            nc.tensor.matmul(
-                acc[piece, m][:], w_emb_sb[k][:, block(m)], embeds_sb[piece][k][:], start=start, stop=stop
-            )
+            moving = embeds0_sb[k][:] if piece == 0 else embeds1_sb[:, k, :]
+            nc.tensor.matmul(acc[piece, m][:], w_emb_sb[k][:, block(m)], moving, start=start, stop=stop)
 
         def project_labels(piece, m, start, stop):
             piece_offsets = offsets[:, piece * (PIECE // 16) : (piece + 1) * (PIECE // 16)]
@@ -100,7 +94,8 @@ def tile_rsaffdecoder_kernel(tc, table, w_lab, embeds, w_emb, query, w_qry, b, o
                 stop=stop,
             )
 
-        def leave_psum(piece, m, parts):
+        def leave_psum(piece, m):
+            parts = END_PARTS if (piece, m) in (banks[0], banks[-1]) else 1
             width = PIECE // parts
             for part in range(parts):
                 first = piece * PIECE + part * width
@@ -126,17 +121,19 @@ def tile_rsaffdecoder_kernel(tc, table, w_lab, embeds, w_emb, query, w_qry, b, o
             for k in range(K_BLOCKS):
                 nc.tensor.matmul(
                     qry_ps[:, m, :],
-                    w_qry_sb[k][:, block(m)],
-                    query_sb[k][:],
+                    w_qry_sb[:, k, block(m)],
+                    query_sb[:, k, :],
                     start=(k == 0),
                     stop=(k == K_BLOCKS - 1),
                 )
-        nc.vector.tensor_tensor(
-            qry_bias[:],
-            qry_ps[:],
-            bias[:].rearrange("p h s -> p (h s)").unsqueeze(2).to_broadcast([P, M_BLOCKS, QUERIES]),
-            ADD,
-        )
+        for h in range(HALVES):
+            of_half = slice(h * STEP, (h + 1) * STEP)
+            nc.vector.tensor_tensor(
+                qry_bias[:, of_half, :],
+                qry_ps[:, of_half, :],
+                bias[h][:].unsqueeze(2).to_broadcast([P, STEP, QUERIES]),
+                ADD,
+            )
 
         for piece, m in banks[M_BLOCKS:EARLY]:
             open_bank(piece, m)
@@ -145,7 +142,7 @@ def tile_rsaffdecoder_kernel(tc, table, w_lab, embeds, w_emb, query, w_qry, b, o
 
         for piece, m in banks[:EARLY]:
             project_labels(piece, m, start=False, stop=True)
-            leave_psum(piece, m, parts=1)
+            leave_psum(piece, m)
         for piece, m in banks[EARLY:]:
             open_bank(piece, m)
             project_labels(piece, m, start=True, stop=False)
@@ -153,4 +150,4 @@ def tile_rsaffdecoder_kernel(tc, table, w_lab, embeds, w_emb, query, w_qry, b, o
         for piece, m in banks[EARLY:]:
             for k in range(K_BLOCKS):
                 project_embeds(piece, m, k, start=False, stop=(k == K_BLOCKS - 1))
-            leave_psum(piece, m, parts=LATE_PARTS)
+            leave_psum(piece, m)

@@ -24,6 +24,7 @@ N_BANKS = PIECES * M_BLOCKS
 EARLY = N_BANKS - 1
 END_PARTS = 2
 WARM_UP = 10
+WARM_ROWS = 32
 
 FLOPS = 2 * FEATS * (N * (P + EMB) + QUERIES * EMB)
 
@@ -61,11 +62,12 @@ def tile_rsaffdecoder_kernel(tc, table, w_lab, embeds, w_emb, query, w_qry, b, o
         nc.sync.dma_start(w_lab_sb[:], w_lab)
         nc.sync.dma_start(table_sb[:], table)
 
-        zeros = held.tile([P, P], BF16, name="zeros")
-        nc.vector.memset(zeros[:], 0.0)
+        zeros = held.tile([P, WARM_ROWS], BF16, name="zeros")
+        nc.gpsimd.memset(zeros[:], 0.0)
         warm_ps = psum.tile([P, PIECE], F32, name="warm_ps", tag="bank")
+        many_zeros = zeros[:].unsqueeze(1).to_broadcast([P, P // WARM_ROWS, WARM_ROWS])
         for i in range(WARM_UP):
-            nc.tensor.matmul(warm_ps[:, 0:P], zeros[:], zeros[:], start=True, stop=True)
+            nc.tensor.matmul(warm_ps[0:WARM_ROWS, 0:P], zeros[:], many_zeros, start=True, stop=True)
 
         banks = [(piece, m) for piece in range(PIECES) for m in range(M_BLOCKS)]
         acc = {}

@@ -63,7 +63,7 @@ def tile_rsaffdecoder_kernel(tc, table, w_lab, embeds, w_emb, query, w_qry, b, o
         nc.sync.dma_start(table_sb[:], table)
 
         zeros = held.tile([P, WARM_ROWS], BF16, name="zeros")
-        nc.gpsimd.memset(zeros[:], 0.0)
+        nc.vector.memset(zeros[:], 0.0)
         warm_ps = psum.tile([P, PIECE], F32, name="warm_ps", tag="bank")
         many_zeros = zeros[:].unsqueeze(1).to_broadcast([P, P // WARM_ROWS, WARM_ROWS])
         for i in range(WARM_UP):

@@ -10,6 +10,7 @@ EMB = 256
 QUERIES = 128
 NEIGH = 8
 N = 1024
+FIRST = 256
 PIECE = 512
 
 M_BLOCKS = FEATS // P
@@ -41,23 +42,23 @@ def tile_rsaffdecoder_kernel(tc, table, w_lab, embeds, w_emb, query, w_qry, b, o
         embeds1_sb = held.tile([P, K_BLOCKS, PIECE], BF16, name="embeds1_sb")
         query_sb = held.tile([P, K_BLOCKS, QUERIES], BF16, name="query_sb")
         w_qry_sb = held.tile([P, K_BLOCKS, FEATS], BF16, name="w_qry_sb")
-        bias = [held.tile([P, STEP], F32, name=f"bias{h}") for h in range(HALVES)]
+        bias = held.tile([P, HALVES, STEP], F32, name="bias")
         offsets = held.tile([P, N // 16], U16, name="offsets")
         w_lab_sb = held.tile([P, FEATS], BF16, name="w_lab_sb")
         table_sb = held.tile([P, LABELS], BF16, name="table_sb")
 
-        nc.sync.dma_start(embeds0_sb[0][:], embeds[0:P, 0:PIECE])
         for h in range(HALVES):
             half = slice(h * HALF, (h + 1) * HALF)
             nc.sync.dma_start(w_emb_sb[0][:, half], w_emb[0:P, half])
+            part = slice(h * FIRST, (h + 1) * FIRST)
+            nc.sync.dma_start(embeds0_sb[0][:, part], embeds[0:P, part])
         nc.sync.dma_start(embeds0_sb[1][:], embeds[P:EMB, 0:PIECE])
         nc.sync.dma_start(w_emb_sb[1][:], w_emb[P:EMB, :])
         nc.sync.dma_start(query_sb[:], query.rearrange("(p k) q -> p k q", k=K_BLOCKS))
         nc.sync.dma_start(w_qry_sb[:], w_qry.rearrange("(p k) f -> p k f", k=K_BLOCKS))
         for k in range(K_BLOCKS):
             nc.sync.dma_start(embeds1_sb[:, k, :], embeds[k * P : (k + 1) * P, PIECE:N])
-        for h in range(HALVES):
-            nc.sync.dma_start(bias[h][:], b[h * HALF : (h + 1) * HALF, :].rearrange("(p s) o -> p (s o)", s=STEP))
+        nc.sync.dma_start(bias[:], b.rearrange("(h p s) o -> p h (s o)", h=HALVES, s=STEP))
         nc.sync.dma_start(offsets[:], offs)
         nc.sync.dma_start(w_lab_sb[:], w_lab)
         nc.sync.dma_start(table_sb[:], table)
@@ -85,6 +86,16 @@ def tile_rsaffdecoder_kernel(tc, table, w_lab, embeds, w_emb, query, w_qry, b, o
         def project_embeds(piece, m, k, start, stop):
             moving = embeds0_sb[k][:] if piece == 0 else embeds1_sb[:, k, :]
             nc.tensor.matmul(acc[piece, m][:], w_emb_sb[k][:, block(m)], moving, start=start, stop=stop)
+
+        def begin_banks(piece, blocks, part):
+            for m in blocks:
+                nc.tensor.matmul(
+                    acc[piece, m][:, part],
+                    w_emb_sb[0][:, block(m)],
+                    embeds0_sb[0][:, part],
+                    start=(part.start == 0),
+                    stop=False,
+                )
 
         def project_labels(piece, m, start, stop):
             piece_offsets = offsets[:, piece * (PIECE // 16) : (piece + 1) * (PIECE // 16)]
@@ -114,9 +125,10 @@ def tile_rsaffdecoder_kernel(tc, table, w_lab, embeds, w_emb, query, w_qry, b, o
 
         for piece, m in banks[:M_BLOCKS]:
             open_bank(piece, m)
-        for k in range(K_BLOCKS):
-            for piece, m in banks[:M_BLOCKS]:
-                project_embeds(piece, m, k, start=(k == 0), stop=False)
+        for i in range(PIECE // FIRST):
+            begin_banks(0, range(M_BLOCKS), slice(i * FIRST, (i + 1) * FIRST))
+        for piece, m in banks[:M_BLOCKS]:
+            project_embeds(piece, m, 1, start=False, stop=False)
 
         qry_ps = psum.tile([P, M_BLOCKS, QUERIES], F32, name="qry_ps", tag="bank")
         for m in range(M_BLOCKS):
@@ -128,14 +140,12 @@ def tile_rsaffdecoder_kernel(tc, table, w_lab, embeds, w_emb, query, w_qry, b, o
                     start=(k == 0),
                     stop=(k == K_BLOCKS - 1),
                 )
-        for h in range(HALVES):
-            of_half = slice(h * STEP, (h + 1) * STEP)
-            nc.vector.tensor_tensor(
-                qry_bias[:, of_half, :],
-                qry_ps[:, of_half, :],
-                bias[h][:].unsqueeze(2).to_broadcast([P, STEP, QUERIES]),
-                ADD,
-            )
+        nc.vector.tensor_tensor(
+            qry_bias[:],
+            qry_ps[:],
+            bias[:].rearrange("p h s -> p (h s)").unsqueeze(2).to_broadcast([P, M_BLOCKS, QUERIES]),
+            ADD,
+        )
 
         for piece, m in banks[M_BLOCKS:EARLY]:
             open_bank(piece, m)

import concourse.mybir as mybir

BF16, F32, U16 = mybir.dt.bfloat16, mybir.dt.float32, mybir.dt.uint16
ADD = mybir.AluOpType.add

P = 128
LABELS = 2048
FEATS = 512
EMB = 256
QUERIES = 128
NEIGH = 8
N = 1024
FIRST = 256
PIECE = 512

M_BLOCKS = FEATS // P
HALVES = 2
HALF = FEATS // HALVES
STEP = M_BLOCKS // HALVES
K_BLOCKS = EMB // P
PIECES = N // PIECE
PSUM_BANKS = 8

N_BANKS = PIECES * M_BLOCKS
EARLY = N_BANKS - 1
END_PARTS = 2
WARM_UP = 10
WARM_ROWS = 32

FLOPS = 2 * FEATS * (N * (P + EMB) + QUERIES * EMB)


def tile_rsaffdecoder_kernel(tc, table, w_lab, embeds, w_emb, query, w_qry, b, offs, out):
    nc = tc.nc
    with (
        tc.tile_pool(name="held", bufs=1) as held,
        tc.tile_pool(name="stage", bufs=N_BANKS - 2 + 2 * END_PARTS) as stage,
        tc.psum_pool(name="psum", bufs=PSUM_BANKS) as psum,
    ):
        w_emb_sb = [held.tile([P, FEATS], BF16, name=f"w_emb_sb{k}") for k in range(K_BLOCKS)]
        embeds0_sb = [held.tile([P, PIECE], BF16, name=f"embeds0_sb{k}") for k in range(K_BLOCKS)]
        embeds1_sb = held.tile([P, K_BLOCKS, PIECE], BF16, name="embeds1_sb")
        query_sb = held.tile([P, K_BLOCKS, QUERIES], BF16, name="query_sb")
        w_qry_sb = held.tile([P, K_BLOCKS, FEATS], BF16, name="w_qry_sb")
        bias = held.tile([P, HALVES, STEP], F32, name="bias")
        offsets = held.tile([P, N // 16], U16, name="offsets")
        w_lab_sb = held.tile([P, FEATS], BF16, name="w_lab_sb")
        table_sb = held.tile([P, LABELS], BF16, name="table_sb")

        for h in range(HALVES):
            half = slice(h * HALF, (h + 1) * HALF)
            nc.sync.dma_start(w_emb_sb[0][:, half], w_emb[0:P, half])
            part = slice(h * FIRST, (h + 1) * FIRST)
            nc.sync.dma_start(embeds0_sb[0][:, part], embeds[0:P, part])
        nc.sync.dma_start(embeds0_sb[1][:], embeds[P:EMB, 0:PIECE])
        nc.sync.dma_start(w_emb_sb[1][:], w_emb[P:EMB, :])
        nc.sync.dma_start(query_sb[:], query.rearrange("(p k) q -> p k q", k=K_BLOCKS))
        nc.sync.dma_start(w_qry_sb[:], w_qry.rearrange("(p k) f -> p k f", k=K_BLOCKS))
        for k in range(K_BLOCKS):
            nc.sync.dma_start(embeds1_sb[:, k, :], embeds[k * P : (k + 1) * P, PIECE:N])
        nc.sync.dma_start(bias[:], b.rearrange("(h p s) o -> p h (s o)", h=HALVES, s=STEP))
        nc.sync.dma_start(offsets[:], offs)
        nc.sync.dma_start(w_lab_sb[:], w_lab)
        nc.sync.dma_start(table_sb[:], table)

        zeros = held.tile([P, WARM_ROWS], BF16, name="zeros")
        nc.vector.memset(zeros[:], 0.0)
        warm_ps = psum.tile([P, PIECE], F32, name="warm_ps", tag="bank")
        many_zeros = zeros[:].unsqueeze(1).to_broadcast([P, P // WARM_ROWS, WARM_ROWS])
        for i in range(WARM_UP):
            nc.tensor.matmul(warm_ps[0:WARM_ROWS, 0:P], zeros[:], many_zeros, start=True, stop=True)

        banks = [(piece, m) for piece in range(PIECES) for m in range(M_BLOCKS)]
        acc = {}
        qry_bias = held.tile([P, M_BLOCKS, QUERIES], F32, name="qry_bias")

        def block(m):
            first = (m // STEP) * HALF + m % STEP
            return slice(first, (m // STEP + 1) * HALF, STEP)

        out_blocks = out.rearrange("(h p s) j -> h s p j", h=HALVES, s=STEP)

        def open_bank(piece, m):
            acc[piece, m] = psum.tile([P, PIECE], F32, name=f"acc{piece}_{m}", tag="bank")

        def project_embeds(piece, m, k, start, stop):
            moving = embeds0_sb[k][:] if piece == 0 else embeds1_sb[:, k, :]
            nc.tensor.matmul(acc[piece, m][:], w_emb_sb[k][:, block(m)], moving, start=start, stop=stop)

        def begin_banks(piece, blocks, part):
            for m in blocks:
                nc.tensor.matmul(
                    acc[piece, m][:, part],
                    w_emb_sb[0][:, block(m)],
                    embeds0_sb[0][:, part],
                    start=(part.start == 0),
                    stop=False,
                )

        def project_labels(piece, m, start, stop):
            piece_offsets = offsets[:, piece * (PIECE // 16) : (piece + 1) * (PIECE // 16)]
            nc.tensor.matmul(
                acc[piece, m][:],
                w_lab_sb[:, block(m)],
                table_sb[:].indirect(piece_offsets),
                start=start,
                stop=stop,
            )

        def leave_psum(piece, m):
            parts = END_PARTS if (piece, m) in (banks[0], banks[-1]) else 1
            width = PIECE // parts
            for part in range(parts):
                first = piece * PIECE + part * width
                staged = stage.tile([P, width], F32, name="staged")
                nc.vector.tensor_tensor(
                    staged[:].rearrange("p (q n) -> p q n", n=NEIGH),
                    acc[piece, m][:, part * width : (part + 1) * width].rearrange("p (q n) -> p q n", n=NEIGH),
                    qry_bias[:, m, first // NEIGH : (first + width) // NEIGH]
                    .unsqueeze(2)
                    .to_broadcast([P, width // NEIGH, NEIGH]),
                    ADD,
                )
                nc.sync.dma_start(out_blocks[m // STEP][m % STEP][:, first : first + width], staged[:])

        for piece, m in banks[:M_BLOCKS]:
            open_bank(piece, m)
        for i in range(PIECE // FIRST):
            begin_banks(0, range(M_BLOCKS), slice(i * FIRST, (i + 1) * FIRST))
        for piece, m in banks[:M_BLOCKS]:
            project_embeds(piece, m, 1, start=False, stop=False)

        qry_ps = psum.tile([P, M_BLOCKS, QUERIES], F32, name="qry_ps", tag="bank")
        for m in range(M_BLOCKS):
            for k in range(K_BLOCKS):
                nc.tensor.matmul(
                    qry_ps[:, m, :],
                    w_qry_sb[:, k, block(m)],
                    query_sb[:, k, :],
                    start=(k == 0),
                    stop=(k == K_BLOCKS - 1),
                )
        nc.vector.tensor_tensor(
            qry_bias[:],
            qry_ps[:],
            bias[:].rearrange("p h s -> p (h s)").unsqueeze(2).to_broadcast([P, M_BLOCKS, QUERIES]),
            ADD,
        )

        for piece, m in banks[M_BLOCKS:EARLY]:
            open_bank(piece, m)
            for k in range(K_BLOCKS):
                project_embeds(piece, m, k, start=(k == 0), stop=False)

        for piece, m in banks[:EARLY]:
            project_labels(piece, m, start=False, stop=True)
            leave_psum(piece, m)
        for piece, m in banks[EARLY:]:
            open_bank(piece, m)
            project_labels(piece, m, start=True, stop=False)

        for piece, m in banks[EARLY:]:
            for k in range(K_BLOCKS):
                project_embeds(piece, m, k, start=False, stop=(k == K_BLOCKS - 1))
            leave_psum(piece, m)
